import numpy as np
import ml_dtypes


def mxq(x, axis, fmt="e4m3"):
    dtype, down = {"e4m3": (ml_dtypes.float8_e4m3fn, 7), "e5m2": (ml_dtypes.float8_e5m2, 14)}[fmt]
    v = np.moveaxis(np.asarray(x, np.float32).astype(ml_dtypes.bfloat16).astype(np.float64), axis, -1)
    blocks = v.reshape(v.shape[:-1] + (-1, 32))
    amax = np.abs(blocks).max(-1, keepdims=True)
    byte = np.maximum(np.where(amax > 0, np.frexp(amax)[1] - 1 + 127, 0) - down, 1)
    scale = np.exp2(byte - 127.0)
    codes = (blocks / scale).astype(np.float32).astype(dtype).astype(np.float64)
    return np.moveaxis((codes * scale).reshape(v.shape), -1, axis)


WIDE = False


def mx_kscale(k):
    if not WIDE:
        return np.ones(k)
    levels = np.array([10, -10, 5, -5, 0])
    if k % 512:
        return np.exp2(np.random.permutation(np.resize(levels, k // 32))).repeat(32)
    a = np.empty((k // 512, 16))
    for p in range(k // 512):
        a[p, :8] = np.random.permutation(np.resize(levels, 8))
        for g in range(8):
            far = levels[np.abs(levels - a[p, g]) >= 10]
            a[p, g + 8] = far[np.random.randint(len(far))]
    return np.exp2(a.ravel()).repeat(32)


BF16 = ml_dtypes.bfloat16


def bf(x):
    return np.asarray(x, np.float32).astype(BF16)


def f64(x):
    return np.asarray(x).astype(np.float64)


B, A, E, P, R = 256, 8, 512, 512, 512


def setup_inputs():
    s_src, s_edge = mx_kscale(E), mx_kscale(E)
    t = mx_kscale(P)
    s_cat = np.concatenate([s_src, s_edge])
    return {
        "image_features": bf(np.random.standard_normal((B, E)) * s_src),
        "edge_attributes": bf(np.random.standard_normal((B, A, E)) * s_edge),
        "linear_w": bf(np.random.standard_normal((P, 2 * E)) / np.sqrt(2 * E) / s_cat * t[:, None]),
        "linear_b": bf(np.random.standard_normal(P) * 0.3 * t),
        "fwd_proj": bf(np.random.standard_normal((A, P, R)) / np.sqrt(P) / t[:, None]),
    }


def reference(image_features, edge_attributes, linear_w, linear_b, fwd_proj):
    w = f64(linear_w)
    node = f64(bf(mxq(f64(image_features), 1, "e4m3") @ mxq(w[:, :E].T, 0, "e4m3")))
    edge = f64(bf(mxq(f64(edge_attributes).reshape(B * A, E), 1, "e4m3") @ mxq(w[:, E:].T, 0, "e4m3"))).reshape(B, A, P)
    agg = node[:, None, :] + edge + f64(linear_b)
    rep = mxq(agg.transpose(1, 0, 2), 2, "e4m3") @ mxq(f64(fwd_proj), 1, "e4m3")
    return rep.transpose(1, 0, 2)

@@ -1,0 +1,301 @@
+from contextlib import ExitStack
+
+import concourse.mybir as mybir
+from concourse.masks import make_identity
+
+F32 = mybir.dt.float32
+BF16 = mybir.dt.bfloat16
+U32 = mybir.dt.uint32
+U8 = mybir.dt.uint8
+FP8X4 = mybir.dt.float8_e4m3fn_x4
+ADD = mybir.AluOpType.add
+
+NB, NA, NE, NP, NR = 256, 8, 512, 512, 512
+FLOPS = 2 * (NB + NB * NA) * NE * NP + 2 * NB * NA * NP * NR
+P = 128
+PACK = 4
+STAGE1_PSUM = BF16
+
+VECTOR_COLUMNS = (288, 288, 288, 288, 192, 192, 0, 0)
+
+VECTOR_FILL = (None, ("interleave", 4), ("interleave", 5), ("quantize", 4), ("quantize", 5), ("quantize", 6), None, ("quantize", 7))
+SCALAR_FILL = (None, 6, None, None, 7, None, None, None)
+
+
+def tile_attributegnn_pa_kernel(tc, image_features, edge_attributes, linear_w, linear_b, fwd_proj, out):
+    nc = tc.nc
+    with ExitStack() as ctx:
+        sb = ctx.enter_context(tc.tile_pool(name="sb", bufs=1))
+        ps = ctx.enter_context(tc.psum_pool(name="ps", bufs=1))
+        ctx.enter_context(tc.manual_schedule())
+
+        ident = sb.tile([P, P], F32, name="ident", tag="ident")
+        make_identity(nc, ident[:])
+        bias_sb = sb.tile([P, PACK], BF16, name="bias_sb", tag="bias_sb")
+        nc.scalar.dma_start(out=bias_sb[:], in_=linear_b.rearrange("(p t) -> p t", t=PACK))
+
+        w_view = linear_w.rearrange("(m t) k -> m t k", t=PACK)
+        edge_view = edge_attributes.rearrange("(g p) a k -> p g a k", p=P)
+        out_view = out.rearrange("(g p) a r -> p g a r", p=P)
+
+        w_raw, w_bank, w_grouped, w_mx = {}, {}, {}, {}
+        i_tiles = {}
+        e_raw, e_bank, e_grouped, e_mx = {}, {}, {}, {}
+        f_raw, f_grouped, f_mx = {}, {}, {}
+        node_psum, node_bias = {}, {}
+        edge_psum, agg_grouped, agg_mx = {}, {}, {}
+        out_psum, out_sb = {}, {}
+
+
+        def load_weights(t):
+            w_raw[t] = sb.tile([P, 2 * NE], BF16, name="w_raw%d" % t, tag="w_raw%d" % t)
+            nc.sync.dma_start(out=w_raw[t][:], in_=w_view[:, t, :])
+
+        def load_image():
+            i_tiles["raw"] = sb.tile([P, 2, NE], BF16, name="i_raw", tag="i_raw")
+            nc.sync.dma_start(out=i_tiles["raw"][:], in_=image_features.rearrange("(g p) k -> p g k", p=P))
+
+        def load_edges(i):
+            e_raw[i] = sb.tile([P, 2, 2, NE], BF16, name="e_raw%d" % i, tag="e_raw%d" % i)
+            nc.sync.dma_start(out=e_raw[i][:], in_=edge_view[:, :, 2 * i : 2 * i + 2, :])
+
+        def load_proj(a):
+            f_raw[a] = sb.tile([P, PACK, NR], BF16, name="f_raw%d" % a, tag="f_raw%d" % a)
+            nc.sync.dma_start(out=f_raw[a][:], in_=fwd_proj[a].rearrange("(p j) r -> p j r", j=PACK))
+
+
+        def transpose_two(sources, name):
+            bank = ps.tile([P, 2, 2, P], F32, name=name, tag="tp", bufs=2)
+            for g in (0, 1):
+                words = sources[g].bitcast(F32)
+                for u in (0, 1):
+                    nc.tensor.transpose(bank[:, g, u, :], words[:, u : NE // 2 : 2], ident[:])
+            return bank
+
+        def copy_grouped(bank, name, tag, bufs):
+            grouped = sb.tile([P, 2, P, PACK], BF16, name=name, tag=tag, bufs=bufs, align_bytes=64)
+            nc.scalar.copy(out=grouped[:].bitcast(F32), in_=bank[:].rearrange("p g u b -> p g b u"))
+            return grouped
+
+        def quantize(grouped_flat, width, name):
+            codes = sb.tile([P, width // PACK], U32, name=name + "_c", tag=name + "_c", align_bytes=64)
+            scales = sb.tile([P, width // PACK], U8, name=name + "_s", tag=name + "_s", align_bytes=64)
+            nc.vector.quantize_mx(out=codes[:].bitcast(FP8X4), scales=scales[:], in_=grouped_flat)
+            return codes, scales
+
+        def one_pass(out_ap, stationary, s_cols, moving, m_cols):
+            nc.tensor.matmul_mx(
+                out=out_ap,
+                lhsT=stationary[0][:, s_cols].bitcast(FP8X4),
+                lhsT_scale=stationary[1][:, s_cols],
+                rhs=moving[0][:, m_cols].bitcast(FP8X4),
+                rhs_scale=moving[1][:, m_cols],
+                start=True,
+                stop=True,
+            )
+
+        def stage1(x_mx, g, half, name):
+            tile = ps.tile([P, PACK, P], STAGE1_PSUM, name=name, tag="s1", bufs=3)
+            for t in range(PACK):
+                one_pass(tile[:, t, :], w_mx[t], slice(half * P, (half + 1) * P), x_mx, slice(g * P, (g + 1) * P))
+            return tile
+
+
+        def transpose_weights(t):
+            w_bank[t] = transpose_two([w_raw[t][:, 0:NE], w_raw[t][:, NE : 2 * NE]], "w_tp")
+
+        def copy_weights(t):
+            w_grouped[t] = copy_grouped(w_bank[t], "w_grp%d" % t, "w_grp%d" % t, 1)
+
+        def quantize_weights(t):
+            w_mx[t] = quantize(w_grouped[t][:].rearrange("p g b j -> p (g b j)"), 2 * P * PACK, "w_q%d" % t)
+
+        def transpose_image():
+            i_tiles["bank"] = transpose_two([i_tiles["raw"][:, 0, :], i_tiles["raw"][:, 1, :]], "i_tp")
+
+        def copy_image():
+            i_tiles["grouped"] = copy_grouped(i_tiles["bank"], "i_grp", "i_grp", 1)
+
+        def quantize_image():
+            i_tiles["mx"] = quantize(i_tiles["grouped"][:].rearrange("p g b j -> p (g b j)"), 2 * P * PACK, "i_q")
+
+        def node_passes(g):
+            node_psum[g] = stage1(i_tiles["mx"], g, 0, "n_bank")
+
+        def node_plus_bias(g):
+            node_bias[g] = sb.tile([P, P, PACK], F32, name="nodeb%d" % g, tag="nodeb%d" % g)
+            nc.vector.tensor_tensor(
+                out=node_bias[g][:],
+                in0=node_psum[g][:].rearrange("p t b -> p b t"),
+                in1=bias_sb[:].unsqueeze(1).to_broadcast([P, P, PACK]),
+                op=ADD,
+            )
+
+
+        def transpose_edges(a):
+            raw = e_raw[a // 2]
+            e_bank[a] = transpose_two([raw[:, 0, a % 2, :], raw[:, 1, a % 2, :]], "e_tp")
+
+        def copy_edges(a):
+            e_grouped[a] = copy_grouped(e_bank[a], "e_grp", "e_grp", 4)
+
+        def quantize_edges(a):
+            e_mx[a] = quantize(e_grouped[a][:].rearrange("p g b j -> p (g b j)"), 2 * P * PACK, "e_q%d" % a)
+
+        def edge_passes(a, g):
+            edge_psum[a, g] = stage1(e_mx[a], g, 1, "e_bank")
+
+        def add_node(a, g):
+            if g == 0:
+                agg_grouped[a] = sb.tile([P, 2, P, PACK], BF16, name="a_grp", tag="a_grp", bufs=3, align_bytes=64)
+            nc.vector.tensor_tensor(
+                out=agg_grouped[a][:, g, :, :],
+                in0=edge_psum[a, g][:].rearrange("p t b -> p b t"),
+                in1=node_bias[g][:],
+                op=ADD,
+            )
+
+        def quantize_agg(a):
+            agg_mx[a] = quantize(agg_grouped[a][:].rearrange("p g b j -> p (g b j)"), 2 * P * PACK, "a_q%d" % a)
+
+
+        def interleave_proj(a, engine_copy, cols):
+            if a not in f_grouped:
+                f_grouped[a] = sb.tile([P, NR, PACK], BF16, name="f_grp%d" % a, tag="f_grp%d" % a, align_bytes=64)
+            engine_copy(out=f_grouped[a][:, cols, :], in_=f_raw[a][:, :, cols].rearrange("p j r -> p r j"))
+
+        def interleave_proj_vector(a):
+            interleave_proj(a, nc.vector.tensor_copy, slice(0, VECTOR_COLUMNS[a]))
+
+        def interleave_proj_scalar(a):
+            interleave_proj(a, nc.scalar.copy, slice(VECTOR_COLUMNS[a], NR))
+
+        def quantize_proj(a):
+            f_mx[a] = quantize(f_grouped[a][:].rearrange("p r j -> p (r j)"), NR * PACK, "f_q%d" % a)
+
+
+        def out_passes(a):
+            for g in (0, 1):
+                out_psum[a, g] = ps.tile([P, NR], F32, name="o_bank", tag="s2", bufs=3)
+                one_pass(out_psum[a, g][:], agg_mx[a], slice(g * P, (g + 1) * P), f_mx[a], slice(0, NR))
+
+        def copy_and_store(a):
+            out_sb[a] = sb.tile([P, 2, NR], F32, name="o_st", tag="o_st", bufs=4)
+            if a < NA - 1:
+                for g in (0, 1):
+                    nc.scalar.copy(out=out_sb[a][:, g, :], in_=out_psum[a, g][:])
+                nc.sync.dma_start(out=out_view[:, :, a, :], in_=out_sb[a][:])
+            else:
+                nc.scalar.copy(out=out_sb[a][:, 0, :], in_=out_psum[a, 0][:])
+                nc.sync.dma_start(out=out_view[:, 0, a, :], in_=out_sb[a][:, 0, :])
+                nc.vector.tensor_copy(out=out_sb[a][:, 1, :], in_=out_psum[a, 1][:])
+                nc.sync.dma_start(out=out_view[:, 1, a, :], in_=out_sb[a][:, 1, :])
+
+        def vector_fill(slot):
+            if VECTOR_FILL[slot] is not None:
+                what, a = VECTOR_FILL[slot]
+                if what == "interleave":
+                    interleave_proj_vector(a)
+                else:
+                    quantize_proj(a)
+
+        def scalar_fill(slot):
+            if SCALAR_FILL[slot] is not None:
+                interleave_proj_scalar(SCALAR_FILL[slot])
+
+        load_weights(0)
+        load_proj(0)
+        load_weights(1)
+        load_weights(2)
+        load_proj(1)
+        load_weights(3)
+        load_image()
+        load_proj(2)
+        load_edges(0)
+        load_proj(3)
+        load_edges(1)
+        load_proj(4)
+        load_proj(5)
+        load_edges(2)
+        load_proj(6)
+        load_proj(7)
+        load_edges(3)
+
+        transpose_weights(0)
+        interleave_proj_scalar(0)
+        interleave_proj_vector(0)
+        copy_weights(0)
+        transpose_weights(1)
+        copy_weights(1)
+        quantize_weights(0)
+        quantize_proj(0)
+        interleave_proj_scalar(1)
+        interleave_proj_vector(1)
+        transpose_weights(2)
+        copy_weights(2)
+        quantize_weights(1)
+        transpose_weights(3)
+        copy_weights(3)
+        quantize_proj(1)
+        quantize_weights(2)
+        interleave_proj_scalar(2)
+        interleave_proj_vector(2)
+        transpose_image()
+        copy_image()
+        quantize_weights(3)
+        quantize_proj(2)
+        interleave_proj_scalar(3)
+        interleave_proj_vector(3)
+        quantize_image()
+        transpose_edges(0)
+        copy_edges(0)
+        transpose_edges(1)
+        copy_edges(1)
+        quantize_proj(3)
+
+        node_passes(0)
+        node_passes(1)
+        quantize_edges(0)
+        quantize_edges(1)
+        node_plus_bias(0)
+        edge_passes(0, 0)
+        node_plus_bias(1)
+        edge_passes(0, 1)
+        edge_passes(1, 0)
+        interleave_proj_scalar(4)
+        interleave_proj_scalar(5)
+        transpose_edges(2)
+        copy_edges(2)
+        transpose_edges(3)
+        copy_edges(3)
+
+        for j in range(NA // 2):
+            first, second = 2 * j, 2 * j + 1
+            vector_fill(2 * j)
+            add_node(first, 0)
+            add_node(first, 1)
+            edge_passes(second, 1)
+            add_node(second, 0)
+            quantize_agg(first)
+            out_passes(first)
+            if first + 4 < NA:
+                transpose_edges(first + 4)
+                transpose_edges(second + 4)
+            copy_and_store(first)
+            if first + 4 < NA:
+                copy_edges(first + 4)
+            scalar_fill(2 * j)
+            add_node(second, 1)
+            vector_fill(2 * j + 1)
+            quantize_agg(second)
+            out_passes(second)
+            copy_and_store(second)
+            if first + 4 < NA:
+                copy_edges(second + 4)
+            scalar_fill(2 * j + 1)
+            if first + 2 < NA:
+                quantize_edges(first + 2)
+                quantize_edges(second + 2)
+                edge_passes(first + 2, 0)
+                edge_passes(first + 2, 1)
+                edge_passes(second + 2, 0)

@@ -162,7 +162,10 @@ def tile_attributegnn_pa_kernel(tc, image_features, edge_attributes, linear_w, l
         def interleave_proj(a, engine_copy, cols):
             if a not in f_grouped:
                 f_grouped[a] = sb.tile([P, NR, PACK], BF16, name="f_grp%d" % a, tag="f_grp%d" % a, align_bytes=64)
-            engine_copy(out=f_grouped[a][:, cols, :], in_=f_raw[a][:, :, cols].rearrange("p j r -> p r j"))
+            engine_copy(
+                out=f_grouped[a][:, cols, :].rearrange("p (c i) j -> p c j i", i=4),
+                in_=f_raw[a][:, :, cols].rearrange("p j (c i) -> p c j i", i=4),
+            )
 
         def interleave_proj_vector(a):
             interleave_proj(a, nc.vector.tensor_copy, slice(0, VECTOR_COLUMNS[a]))

@@ -9,6 +9,7 @@ U32 = mybir.dt.uint32
 U8 = mybir.dt.uint8
 FP8X4 = mybir.dt.float8_e4m3fn_x4
 ADD = mybir.AluOpType.add
+MULT = mybir.AluOpType.mult
 
 NB, NA, NE, NP, NR = 256, 8, 512, 512, 512
 FLOPS = 2 * (NB + NB * NA) * NE * NP + 2 * NB * NA * NP * NR
@@ -16,10 +17,12 @@ P = 128
 PACK = 4
 STAGE1_PSUM = BF16
 
-VECTOR_COLUMNS = (288, 288, 288, 288, 192, 192, 0, 0)
+HEAD_VECTOR_0, HEAD_VECTOR_1 = 256, 320
 
-VECTOR_FILL = (None, ("interleave", 4), ("interleave", 5), ("quantize", 4), ("quantize", 5), ("quantize", 6), None, ("quantize", 7))
-SCALAR_FILL = (None, 6, None, None, 7, None, None, None)
+HEAD_PARTS = (("vector", 0, HEAD_VECTOR_0), ("scalar", HEAD_VECTOR_0, NR))
+HEAD_PARTS_1 = (("vector", 0, HEAD_VECTOR_1), ("scalar", HEAD_VECTOR_1, NR))
+LOOP_PARTS = (("gpsimd", 0, 128), ("tensor", 128, 384), ("vector", 384, 448), ("scalar", 448, NR))
+PARTS = (HEAD_PARTS, HEAD_PARTS_1) + (LOOP_PARTS,) * 6
 
 
 def tile_attributegnn_pa_kernel(tc, image_features, edge_attributes, linear_w, linear_b, fwd_proj, out):
@@ -31,6 +34,8 @@ def tile_attributegnn_pa_kernel(tc, image_features, edge_attributes, linear_w, l
 
         ident = sb.tile([P, P], F32, name="ident", tag="ident")
         make_identity(nc, ident[:])
+        ident_bf = sb.tile([P, P], BF16, name="ident_bf", tag="ident_bf")
+        make_identity(nc, ident_bf[:])
         bias_sb = sb.tile([P, PACK], BF16, name="bias_sb", tag="bias_sb")
         nc.scalar.dma_start(out=bias_sb[:], in_=linear_b.rearrange("(p t) -> p t", t=PACK))
 
@@ -41,8 +46,8 @@ def tile_attributegnn_pa_kernel(tc, image_features, edge_attributes, linear_w, l
         w_raw, w_bank, w_grouped, w_mx = {}, {}, {}, {}
         i_tiles = {}
         e_raw, e_bank, e_grouped, e_mx = {}, {}, {}, {}
-        f_raw, f_grouped, f_mx = {}, {}, {}
-        node_psum, node_bias = {}, {}
+        f_raw, f_bank, f_grouped, f_mx = {}, {}, {}, {}
+        node_tiles = {}
         edge_psum, agg_grouped, agg_mx = {}, {}, {}
         out_psum, out_sb = {}, {}
 
@@ -65,7 +70,7 @@ def tile_attributegnn_pa_kernel(tc, image_features, edge_attributes, linear_w, l
 
 
         def transpose_two(sources, name):
-            bank = ps.tile([P, 2, 2, P], F32, name=name, tag="tp", bufs=2)
+            bank = ps.tile([P, 2, 2, P], F32, name=name, tag="tp", bufs=3)
             for g in (0, 1):
                 words = sources[g].bitcast(F32)
                 for u in (0, 1):
@@ -94,10 +99,10 @@ def tile_attributegnn_pa_kernel(tc, image_features, edge_attributes, linear_w, l
                 stop=True,
             )
 
-        def stage1(x_mx, g, half, name):
-            tile = ps.tile([P, PACK, P], STAGE1_PSUM, name=name, tag="s1", bufs=3)
+        def stage1(x_mx, half, name):
+            tile = ps.tile([P, PACK, NB], STAGE1_PSUM, name=name, tag="s1", bufs=2)
             for t in range(PACK):
-                one_pass(tile[:, t, :], w_mx[t], slice(half * P, (half + 1) * P), x_mx, slice(g * P, (g + 1) * P))
+                one_pass(tile[:, t, :], w_mx[t], slice(half * P, (half + 1) * P), x_mx, slice(0, NB))
             return tile
 
 
@@ -119,15 +124,15 @@ def tile_attributegnn_pa_kernel(tc, image_features, edge_attributes, linear_w, l
         def quantize_image():
             i_tiles["mx"] = quantize(i_tiles["grouped"][:].rearrange("p g b j -> p (g b j)"), 2 * P * PACK, "i_q")
 
-        def node_passes(g):
-            node_psum[g] = stage1(i_tiles["mx"], g, 0, "n_bank")
+        def node_passes():
+            node_tiles["psum"] = stage1(i_tiles["mx"], 0, "n_bank")
 
-        def node_plus_bias(g):
-            node_bias[g] = sb.tile([P, P, PACK], F32, name="nodeb%d" % g, tag="nodeb%d" % g)
+        def node_plus_bias():
+            node_tiles["bias"] = sb.tile([P, NB, PACK], F32, name="nodeb", tag="nodeb")
             nc.vector.tensor_tensor(
-                out=node_bias[g][:],
-                in0=node_psum[g][:].rearrange("p t b -> p b t"),
-                in1=bias_sb[:].unsqueeze(1).to_broadcast([P, P, PACK]),
+                out=node_tiles["bias"][:],
+                in0=node_tiles["psum"][:].rearrange("p t b -> p b t"),
+                in1=bias_sb[:].unsqueeze(1).to_broadcast([P, NB, PACK]),
                 op=ADD,
             )
 
@@ -142,45 +147,92 @@ def tile_attributegnn_pa_kernel(tc, image_features, edge_attributes, linear_w, l
         def quantize_edges(a):
             e_mx[a] = quantize(e_grouped[a][:].rearrange("p g b j -> p (g b j)"), 2 * P * PACK, "e_q%d" % a)
 
-        def edge_passes(a, g):
-            edge_psum[a, g] = stage1(e_mx[a], g, 1, "e_bank")
+        def edge_passes(a):
+            edge_psum[a] = stage1(e_mx[a], 1, "e_bank")
 
-        def add_node(a, g):
-            if g == 0:
-                agg_grouped[a] = sb.tile([P, 2, P, PACK], BF16, name="a_grp", tag="a_grp", bufs=3, align_bytes=64)
+        def add_node(a):
+            agg_grouped[a] = sb.tile([P, NB, PACK], BF16, name="a_grp", tag="a_grp", bufs=3, align_bytes=64)
             nc.vector.tensor_tensor(
-                out=agg_grouped[a][:, g, :, :],
-                in0=edge_psum[a, g][:].rearrange("p t b -> p b t"),
-                in1=node_bias[g][:],
+                out=agg_grouped[a][:],
+                in0=edge_psum[a][:].rearrange("p t b -> p b t"),
+                in1=node_tiles["bias"][:],
                 op=ADD,
             )
 
         def quantize_agg(a):
-            agg_mx[a] = quantize(agg_grouped[a][:].rearrange("p g b j -> p (g b j)"), 2 * P * PACK, "a_q%d" % a)
+            both = quantize(agg_grouped[a][:].rearrange("p b j -> p (b j)"), NB * PACK, "a_q%d" % a)
+            for g in (0, 1):
+                agg_mx[a, g] = (both, slice(g * P, (g + 1) * P))
 
-
-        def interleave_proj(a, engine_copy, cols):
-            if a not in f_grouped:
-                f_grouped[a] = sb.tile([P, NR, PACK], BF16, name="f_grp%d" % a, tag="f_grp%d" % a, align_bytes=64)
-            engine_copy(
-                out=f_grouped[a][:, cols, :].rearrange("p (c i) j -> p c j i", i=4),
-                in_=f_raw[a][:, :, cols].rearrange("p j (c i) -> p c j i", i=4),
+        def add_node_half(a, g):
+            if g == 0:
+                agg_grouped[a] = sb.tile([P, NB, PACK], BF16, name="a_grp", tag="a_grp", bufs=3, align_bytes=64)
+            nc.vector.tensor_tensor(
+                out=agg_grouped[a][:, g * P : (g + 1) * P, :],
+                in0=edge_psum[a][:, :, g * P : (g + 1) * P].rearrange("p t b -> p b t"),
+                in1=node_tiles["bias"][:, g * P : (g + 1) * P, :],
+                op=ADD,
             )
 
-        def interleave_proj_vector(a):
-            interleave_proj(a, nc.vector.tensor_copy, slice(0, VECTOR_COLUMNS[a]))
+        def quantize_agg_half(a, g):
+            half = agg_grouped[a][:, g * P : (g + 1) * P, :].rearrange("p b j -> p (b j)")
+            agg_mx[a, g] = (quantize(half, P * PACK, "a_q%d%d" % (a, g)), slice(0, P))
 
-        def interleave_proj_scalar(a):
-            interleave_proj(a, nc.scalar.copy, slice(VECTOR_COLUMNS[a], NR))
+
+        def proj_tile(a):
+            if a not in f_grouped:
+                f_grouped[a] = sb.tile([P, NR, PACK], BF16, name="f_grp", tag="f_grp", bufs=2, align_bytes=64)
+            return f_grouped[a]
+
+        def interleave_copy(a, engine_copy, r0, r1):
+            engine_copy(
+                out=proj_tile(a)[:, r0:r1, :].rearrange("p (c i) j -> p c j i", i=4),
+                in_=f_raw[a][:, :, r0:r1].rearrange("p j (c i) -> p c j i", i=4),
+            )
+
+        def proj_parts(a, engine):
+            return [(r0, r1) for who, r0, r1 in PARTS[a] if who == engine]
+
+        def proj_gpsimd(a):
+            for r0, r1 in proj_parts(a, "gpsimd"):
+                nc.gpsimd.tensor_scalar(
+                    out=proj_tile(a)[:, r0:r1, :],
+                    in0=f_raw[a][:, :, r0:r1].rearrange("p j r -> p r j"),
+                    scalar1=1.0,
+                    scalar2=0.0,
+                    op0=MULT,
+                    op1=ADD,
+                )
+
+        def proj_tensor(a):
+            for r0, r1 in proj_parts(a, "tensor"):
+                f_bank[a] = ps.tile([P, r1 - r0, PACK], BF16, name="f_bank", tag="fi", bufs=1)
+                for h in range(0, r1 - r0, P):
+                    nc.tensor.matmul(
+                        out=f_bank[a][:, h : h + P, :],
+                        lhsT=ident_bf[:],
+                        rhs=f_raw[a][:, :, r0 + h : r0 + h + P].rearrange("p j r -> p r j"),
+                        start=True,
+                        stop=True,
+                    )
+
+        def proj_vector(a):
+            for r0, r1 in proj_parts(a, "vector"):
+                interleave_copy(a, nc.vector.tensor_copy, r0, r1)
+
+        def proj_scalar(a):
+            for r0, r1 in proj_parts(a, "tensor"):
+                nc.scalar.copy(out=proj_tile(a)[:, r0:r1, :], in_=f_bank[a][:])
+            for r0, r1 in proj_parts(a, "scalar"):
+                interleave_copy(a, nc.scalar.copy, r0, r1)
 
         def quantize_proj(a):
             f_mx[a] = quantize(f_grouped[a][:].rearrange("p r j -> p (r j)"), NR * PACK, "f_q%d" % a)
 
 
-        def out_passes(a):
-            for g in (0, 1):
-                out_psum[a, g] = ps.tile([P, NR], F32, name="o_bank", tag="s2", bufs=3)
-                one_pass(out_psum[a, g][:], agg_mx[a], slice(g * P, (g + 1) * P), f_mx[a], slice(0, NR))
+        def out_pass(a, g):
+            out_psum[a, g] = ps.tile([P, NR], F32, name="o_bank", tag="s2", bufs=2)
+            one_pass(out_psum[a, g][:], agg_mx[a, g][0], agg_mx[a, g][1], f_mx[a], slice(0, NR))
 
         def copy_and_store(a):
             out_sb[a] = sb.tile([P, 2, NR], F32, name="o_st", tag="o_st", bufs=4)
@@ -194,111 +246,73 @@ def tile_attributegnn_pa_kernel(tc, image_features, edge_attributes, linear_w, l
                 nc.vector.tensor_copy(out=out_sb[a][:, 1, :], in_=out_psum[a, 1][:])
                 nc.sync.dma_start(out=out_view[:, 1, a, :], in_=out_sb[a][:, 1, :])
 
-        def vector_fill(slot):
-            if VECTOR_FILL[slot] is not None:
-                what, a = VECTOR_FILL[slot]
-                if what == "interleave":
-                    interleave_proj_vector(a)
-                else:
-                    quantize_proj(a)
-
-        def scalar_fill(slot):
-            if SCALAR_FILL[slot] is not None:
-                interleave_proj_scalar(SCALAR_FILL[slot])
-
-        load_weights(0)
-        load_proj(0)
-        load_weights(1)
-        load_weights(2)
-        load_proj(1)
-        load_weights(3)
+        for t in range(PACK):
+            load_weights(t)
         load_image()
-        load_proj(2)
         load_edges(0)
-        load_proj(3)
-        load_edges(1)
-        load_proj(4)
-        load_proj(5)
-        load_edges(2)
-        load_proj(6)
-        load_proj(7)
-        load_edges(3)
+        load_proj(0)
+        load_proj(1)
+        for i in (1, 2, 3):
+            load_edges(i)
+            load_proj(2 * i)
+            load_proj(2 * i + 1)
 
-        transpose_weights(0)
-        interleave_proj_scalar(0)
-        interleave_proj_vector(0)
-        copy_weights(0)
-        transpose_weights(1)
-        copy_weights(1)
-        quantize_weights(0)
-        quantize_proj(0)
-        interleave_proj_scalar(1)
-        interleave_proj_vector(1)
-        transpose_weights(2)
-        copy_weights(2)
-        quantize_weights(1)
-        transpose_weights(3)
-        copy_weights(3)
-        quantize_proj(1)
-        quantize_weights(2)
-        interleave_proj_scalar(2)
-        interleave_proj_vector(2)
+        for t in range(PACK):
+            transpose_weights(t)
+            copy_weights(t)
+            quantize_weights(t)
         transpose_image()
         copy_image()
-        quantize_weights(3)
-        quantize_proj(2)
-        interleave_proj_scalar(3)
-        interleave_proj_vector(3)
         quantize_image()
         transpose_edges(0)
         copy_edges(0)
         transpose_edges(1)
         copy_edges(1)
-        quantize_proj(3)
-
-        node_passes(0)
-        node_passes(1)
+        node_passes()
+        proj_vector(0)
+        proj_scalar(0)
         quantize_edges(0)
+        edge_passes(0)
+        node_plus_bias()
         quantize_edges(1)
-        node_plus_bias(0)
-        edge_passes(0, 0)
-        node_plus_bias(1)
-        edge_passes(0, 1)
-        edge_passes(1, 0)
-        interleave_proj_scalar(4)
-        interleave_proj_scalar(5)
+        edge_passes(1)
         transpose_edges(2)
-        copy_edges(2)
         transpose_edges(3)
-        copy_edges(3)
+        proj_vector(1)
+        copy_edges(2)
+        proj_scalar(1)
+        quantize_proj(0)
+        proj_tensor(2)
 
-        for j in range(NA // 2):
-            first, second = 2 * j, 2 * j + 1
-            vector_fill(2 * j)
-            add_node(first, 0)
-            add_node(first, 1)
-            edge_passes(second, 1)
-            add_node(second, 0)
-            quantize_agg(first)
-            out_passes(first)
-            if first + 4 < NA:
-                transpose_edges(first + 4)
-                transpose_edges(second + 4)
-            copy_and_store(first)
-            if first + 4 < NA:
-                copy_edges(first + 4)
-            scalar_fill(2 * j)
-            add_node(second, 1)
-            vector_fill(2 * j + 1)
-            quantize_agg(second)
-            out_passes(second)
-            copy_and_store(second)
-            if first + 4 < NA:
-                copy_edges(second + 4)
-            scalar_fill(2 * j + 1)
-            if first + 2 < NA:
-                quantize_edges(first + 2)
-                quantize_edges(second + 2)
-                edge_passes(first + 2, 0)
-                edge_passes(first + 2, 1)
-                edge_passes(second + 2, 0)
+        for a in range(NA - 1):
+            add_node(a)
+            if a + 2 < NA:
+                proj_gpsimd(a + 2)
+                quantize_edges(a + 2)
+                edge_passes(a + 2)
+                proj_vector(a + 2)
+            if a == NA - 2:
+                quantize_proj(NA - 1)
+            quantize_agg(a)
+            out_pass(a, 0)
+            out_pass(a, 1)
+            if a + 3 < NA:
+                copy_edges(a + 3)
+            if a + 2 < NA:
+                proj_scalar(a + 2)
+            if a + 3 < NA:
+                proj_tensor(a + 3)
+            if a % 2 == 0 and a + 4 < NA:
+                transpose_edges(a + 4)
+                transpose_edges(a + 5)
+            copy_and_store(a)
+            if a + 1 < NA - 1:
+                quantize_proj(a + 1)
+
+        add_node_half(NA - 1, 0)
+        add_node_half(NA - 1, 1)
+        quantize_agg_half(NA - 1, 0)
+        out_pass(NA - 1, 0)
+        quantize_agg_half(NA - 1, 1)
+        out_pass(NA - 1, 1)
+        copy_and_store(NA - 1)

@@ -17,7 +17,7 @@ P = 128
 PACK = 4
 STAGE1_PSUM = BF16
 
-HEAD_VECTOR_0, HEAD_VECTOR_1 = 256, 320
+HEAD_VECTOR_0, HEAD_VECTOR_1 = 256, 192
 
 HEAD_PARTS = (("vector", 0, HEAD_VECTOR_0), ("scalar", HEAD_VECTOR_0, NR))
 HEAD_PARTS_1 = (("vector", 0, HEAD_VECTOR_1), ("scalar", HEAD_VECTOR_1, NR))
@@ -273,14 +273,14 @@ def tile_attributegnn_pa_kernel(tc, image_features, edge_attributes, linear_w, l
         proj_scalar(0)
         quantize_edges(0)
         edge_passes(0)
-        node_plus_bias()
-        quantize_edges(1)
-        edge_passes(1)
         transpose_edges(2)
         transpose_edges(3)
         proj_vector(1)
-        copy_edges(2)
         proj_scalar(1)
+        node_plus_bias()
+        quantize_edges(1)
+        edge_passes(1)
+        copy_edges(2)
         quantize_proj(0)
         proj_tensor(2)
 

@@ -231,20 +231,25 @@ def tile_attributegnn_pa_kernel(tc, image_features, edge_attributes, linear_w, l
 
 
         def out_pass(a, g):
-            out_psum[a, g] = ps.tile([P, NR], F32, name="o_bank", tag="s2", bufs=2)
+            if a < NA - 1:
+                out_psum[a, g] = ps.tile([P, NR], F32, name="o_bank", tag="s2", bufs=2)
+            else:
+                out_psum[a, g] = ps.tile([P, NR], F32, name="o_last", tag="tp", bufs=3)
             one_pass(out_psum[a, g][:], agg_mx[a, g][0], agg_mx[a, g][1], f_mx[a], slice(0, NR))
 
         def copy_and_store(a):
             out_sb[a] = sb.tile([P, 2, NR], F32, name="o_st", tag="o_st", bufs=4)
-            if a < NA - 1:
+            if a < NA - 2:
                 for g in (0, 1):
                     nc.scalar.copy(out=out_sb[a][:, g, :], in_=out_psum[a, g][:])
                 nc.sync.dma_start(out=out_view[:, :, a, :], in_=out_sb[a][:])
             else:
-                nc.scalar.copy(out=out_sb[a][:, 0, :], in_=out_psum[a, 0][:])
-                nc.sync.dma_start(out=out_view[:, 0, a, :], in_=out_sb[a][:, 0, :])
-                nc.vector.tensor_copy(out=out_sb[a][:, 1, :], in_=out_psum[a, 1][:])
-                nc.sync.dma_start(out=out_view[:, 1, a, :], in_=out_sb[a][:, 1, :])
+                for g in (0, 1):
+                    if a == NA - 1 and g == 0:
+                        nc.vector.tensor_copy(out=out_sb[a][:, g, :], in_=out_psum[a, g][:])
+                    else:
+                        nc.scalar.copy(out=out_sb[a][:, g, :], in_=out_psum[a, g][:])
+                    nc.sync.dma_start(out=out_view[:, g, a, :], in_=out_sb[a][:, g, :])
 
         for t in range(PACK):
             load_weights(t)

@@ -22,7 +22,8 @@ HEAD_VECTOR_0, HEAD_VECTOR_1 = 256, 192
 HEAD_PARTS = (("vector", 0, HEAD_VECTOR_0), ("scalar", HEAD_VECTOR_0, NR))
 HEAD_PARTS_1 = (("vector", 0, HEAD_VECTOR_1), ("scalar", HEAD_VECTOR_1, NR))
 LOOP_PARTS = (("gpsimd", 0, 128), ("tensor", 128, 384), ("vector", 384, 448), ("scalar", 448, NR))
-PARTS = (HEAD_PARTS, HEAD_PARTS_1) + (LOOP_PARTS,) * 6
+PLAIN_PARTS = (("gpsimd", 0, 128), ("vector", 128, 256), ("scalar", 256, NR))
+PARTS = (HEAD_PARTS, HEAD_PARTS_1, LOOP_PARTS, PLAIN_PARTS) + (LOOP_PARTS,) * 4
 
 
 def tile_attributegnn_pa_kernel(tc, image_features, edge_attributes, linear_w, linear_b, fwd_proj, out):

@@ -23,7 +23,7 @@ HEAD_PARTS = (("vector", 0, HEAD_VECTOR_0), ("scalar", HEAD_VECTOR_0, NR))
 HEAD_PARTS_1 = (("vector", 0, HEAD_VECTOR_1), ("scalar", HEAD_VECTOR_1, NR))
 LOOP_PARTS = (("gpsimd", 0, 128), ("tensor", 128, 384), ("vector", 384, 448), ("scalar", 448, NR))
 PLAIN_PARTS = (("gpsimd", 0, 128), ("vector", 128, 256), ("scalar", 256, NR))
-PARTS = (HEAD_PARTS, HEAD_PARTS_1, LOOP_PARTS, PLAIN_PARTS) + (LOOP_PARTS,) * 4
+PARTS = (HEAD_PARTS, HEAD_PARTS_1, PLAIN_PARTS, PLAIN_PARTS) + (LOOP_PARTS,) * 4
 
 
 def tile_attributegnn_pa_kernel(tc, image_features, edge_attributes, linear_w, linear_b, fwd_proj, out):

@@ -223,7 +223,10 @@ def tile_attributegnn_pa_kernel(tc, image_features, edge_attributes, linear_w, l
 
         def proj_scalar(a):
             for r0, r1 in proj_parts(a, "tensor"):
-                nc.scalar.copy(out=proj_tile(a)[:, r0:r1, :], in_=f_bank[a][:])
+                nc.scalar.copy(
+                    out=proj_tile(a)[:, r0:r1, :].rearrange("p r j -> p (r j)").bitcast(F32),
+                    in_=f_bank[a][:].rearrange("p r j -> p (r j)").bitcast(F32),
+                )
             for r0, r1 in proj_parts(a, "scalar"):
                 interleave_copy(a, nc.scalar.copy, r0, r1)
 

@@ -210,9 +210,9 @@ def tile_attributegnn_pa_kernel(tc, image_features, edge_attributes, linear_w, l
                 f_bank[a] = ps.tile([P, r1 - r0, PACK], BF16, name="f_bank", tag="fi", bufs=1)
                 for h in range(0, r1 - r0, P):
                     nc.tensor.matmul(
-                        out=f_bank[a][:, h : h + P, :],
+                        out=f_bank[a][:, h : h + P, :].rearrange("p r j -> p j r"),
                         lhsT=ident_bf[:],
-                        rhs=f_raw[a][:, :, r0 + h : r0 + h + P].rearrange("p j r -> p r j"),
+                        rhs=f_raw[a][:, :, r0 + h : r0 + h + P],
                         start=True,
                         stop=True,
                     )

@@ -23,7 +23,7 @@ HEAD_PARTS = (("vector", 0, HEAD_VECTOR_0), ("scalar", HEAD_VECTOR_0, NR))
 HEAD_PARTS_1 = (("vector", 0, HEAD_VECTOR_1), ("scalar", HEAD_VECTOR_1, NR))
 LOOP_PARTS = (("gpsimd", 0, 128), ("tensor", 128, 384), ("vector", 384, 448), ("scalar", 448, NR))
 PLAIN_PARTS = (("gpsimd", 0, 128), ("vector", 128, 256), ("scalar", 256, NR))
-PARTS = (HEAD_PARTS, HEAD_PARTS_1, PLAIN_PARTS, PLAIN_PARTS) + (LOOP_PARTS,) * 4
+PARTS = (HEAD_PARTS, HEAD_PARTS_1, LOOP_PARTS, PLAIN_PARTS) + (LOOP_PARTS,) * 4
 
 
 def tile_attributegnn_pa_kernel(tc, image_features, edge_attributes, linear_w, linear_b, fwd_proj, out):

@@ -235,7 +235,7 @@ def tile_attributegnn_pa_kernel(tc, image_features, edge_attributes, linear_w, l
 
 
         def out_pass(a, g):
-            if a < NA - 1:
+            if a not in (4, 6):
                 out_psum[a, g] = ps.tile([P, NR], F32, name="o_bank", tag="s2", bufs=2)
             else:
                 out_psum[a, g] = ps.tile([P, NR], F32, name="o_last", tag="tp", bufs=3)

from contextlib import ExitStack

import concourse.mybir as mybir
from concourse.masks import make_identity

F32 = mybir.dt.float32
BF16 = mybir.dt.bfloat16
U32 = mybir.dt.uint32
U8 = mybir.dt.uint8
FP8X4 = mybir.dt.float8_e4m3fn_x4
ADD = mybir.AluOpType.add
MULT = mybir.AluOpType.mult

NB, NA, NE, NP, NR = 256, 8, 512, 512, 512
FLOPS = 2 * (NB + NB * NA) * NE * NP + 2 * NB * NA * NP * NR
P = 128
PACK = 4
STAGE1_PSUM = BF16

HEAD_VECTOR_0, HEAD_VECTOR_1 = 256, 192

HEAD_PARTS = (("vector", 0, HEAD_VECTOR_0), ("scalar", HEAD_VECTOR_0, NR))
HEAD_PARTS_1 = (("vector", 0, HEAD_VECTOR_1), ("scalar", HEAD_VECTOR_1, NR))
LOOP_PARTS = (("gpsimd", 0, 128), ("tensor", 128, 384), ("vector", 384, 448), ("scalar", 448, NR))
PLAIN_PARTS = (("gpsimd", 0, 128), ("vector", 128, 256), ("scalar", 256, NR))
PARTS = (HEAD_PARTS, HEAD_PARTS_1, LOOP_PARTS, PLAIN_PARTS) + (LOOP_PARTS,) * 4


def tile_attributegnn_pa_kernel(tc, image_features, edge_attributes, linear_w, linear_b, fwd_proj, out):
    nc = tc.nc
    with ExitStack() as ctx:
        sb = ctx.enter_context(tc.tile_pool(name="sb", bufs=1))
        ps = ctx.enter_context(tc.psum_pool(name="ps", bufs=1))
        ctx.enter_context(tc.manual_schedule())

        ident = sb.tile([P, P], F32, name="ident", tag="ident")
        make_identity(nc, ident[:])
        ident_bf = sb.tile([P, P], BF16, name="ident_bf", tag="ident_bf")
        make_identity(nc, ident_bf[:])
        bias_sb = sb.tile([P, PACK], BF16, name="bias_sb", tag="bias_sb")
        nc.scalar.dma_start(out=bias_sb[:], in_=linear_b.rearrange("(p t) -> p t", t=PACK))

        w_view = linear_w.rearrange("(m t) k -> m t k", t=PACK)
        edge_view = edge_attributes.rearrange("(g p) a k -> p g a k", p=P)
        out_view = out.rearrange("(g p) a r -> p g a r", p=P)

        w_raw, w_bank, w_grouped, w_mx = {}, {}, {}, {}
        i_tiles = {}
        e_raw, e_bank, e_grouped, e_mx = {}, {}, {}, {}
        f_raw, f_bank, f_grouped, f_mx = {}, {}, {}, {}
        node_tiles = {}
        edge_psum, agg_grouped, agg_mx = {}, {}, {}
        out_psum, out_sb = {}, {}


        def load_weights(t):
            w_raw[t] = sb.tile([P, 2 * NE], BF16, name="w_raw%d" % t, tag="w_raw%d" % t)
            nc.sync.dma_start(out=w_raw[t][:], in_=w_view[:, t, :])

        def load_image():
            i_tiles["raw"] = sb.tile([P, 2, NE], BF16, name="i_raw", tag="i_raw")
            nc.sync.dma_start(out=i_tiles["raw"][:], in_=image_features.rearrange("(g p) k -> p g k", p=P))

        def load_edges(i):
            e_raw[i] = sb.tile([P, 2, 2, NE], BF16, name="e_raw%d" % i, tag="e_raw%d" % i)
            nc.sync.dma_start(out=e_raw[i][:], in_=edge_view[:, :, 2 * i : 2 * i + 2, :])

        def load_proj(a):
            f_raw[a] = sb.tile([P, PACK, NR], BF16, name="f_raw%d" % a, tag="f_raw%d" % a)
            nc.sync.dma_start(out=f_raw[a][:], in_=fwd_proj[a].rearrange("(p j) r -> p j r", j=PACK))


        def transpose_two(sources, name):
            bank = ps.tile([P, 2, 2, P], F32, name=name, tag="tp", bufs=3)
            for g in (0, 1):
                words = sources[g].bitcast(F32)
                for u in (0, 1):
                    nc.tensor.transpose(bank[:, g, u, :], words[:, u : NE // 2 : 2], ident[:])
            return bank

        def copy_grouped(bank, name, tag, bufs):
            grouped = sb.tile([P, 2, P, PACK], BF16, name=name, tag=tag, bufs=bufs, align_bytes=64)
            nc.scalar.copy(out=grouped[:].bitcast(F32), in_=bank[:].rearrange("p g u b -> p g b u"))
            return grouped

        def quantize(grouped_flat, width, name):
            codes = sb.tile([P, width // PACK], U32, name=name + "_c", tag=name + "_c", align_bytes=64)
            scales = sb.tile([P, width // PACK], U8, name=name + "_s", tag=name + "_s", align_bytes=64)
            nc.vector.quantize_mx(out=codes[:].bitcast(FP8X4), scales=scales[:], in_=grouped_flat)
            return codes, scales

        def one_pass(out_ap, stationary, s_cols, moving, m_cols):
            nc.tensor.matmul_mx(
                out=out_ap,
                lhsT=stationary[0][:, s_cols].bitcast(FP8X4),
                lhsT_scale=stationary[1][:, s_cols],
                rhs=moving[0][:, m_cols].bitcast(FP8X4),
                rhs_scale=moving[1][:, m_cols],
                start=True,
                stop=True,
            )

        def stage1(x_mx, half, name):
            tile = ps.tile([P, PACK, NB], STAGE1_PSUM, name=name, tag="s1", bufs=2)
            for t in range(PACK):
                one_pass(tile[:, t, :], w_mx[t], slice(half * P, (half + 1) * P), x_mx, slice(0, NB))
            return tile


        def transpose_weights(t):
            w_bank[t] = transpose_two([w_raw[t][:, 0:NE], w_raw[t][:, NE : 2 * NE]], "w_tp")

        def copy_weights(t):
            w_grouped[t] = copy_grouped(w_bank[t], "w_grp%d" % t, "w_grp%d" % t, 1)

        def quantize_weights(t):
            w_mx[t] = quantize(w_grouped[t][:].rearrange("p g b j -> p (g b j)"), 2 * P * PACK, "w_q%d" % t)

        def transpose_image():
            i_tiles["bank"] = transpose_two([i_tiles["raw"][:, 0, :], i_tiles["raw"][:, 1, :]], "i_tp")

        def copy_image():
            i_tiles["grouped"] = copy_grouped(i_tiles["bank"], "i_grp", "i_grp", 1)

        def quantize_image():
            i_tiles["mx"] = quantize(i_tiles["grouped"][:].rearrange("p g b j -> p (g b j)"), 2 * P * PACK, "i_q")

        def node_passes():
            node_tiles["psum"] = stage1(i_tiles["mx"], 0, "n_bank")

        def node_plus_bias():
            node_tiles["bias"] = sb.tile([P, NB, PACK], F32, name="nodeb", tag="nodeb")
            nc.vector.tensor_tensor(
                out=node_tiles["bias"][:],
                in0=node_tiles["psum"][:].rearrange("p t b -> p b t"),
                in1=bias_sb[:].unsqueeze(1).to_broadcast([P, NB, PACK]),
                op=ADD,
            )


        def transpose_edges(a):
            raw = e_raw[a // 2]
            e_bank[a] = transpose_two([raw[:, 0, a % 2, :], raw[:, 1, a % 2, :]], "e_tp")

        def copy_edges(a):
            e_grouped[a] = copy_grouped(e_bank[a], "e_grp", "e_grp", 4)

        def quantize_edges(a):
            e_mx[a] = quantize(e_grouped[a][:].rearrange("p g b j -> p (g b j)"), 2 * P * PACK, "e_q%d" % a)

        def edge_passes(a):
            edge_psum[a] = stage1(e_mx[a], 1, "e_bank")

        def add_node(a):
            agg_grouped[a] = sb.tile([P, NB, PACK], BF16, name="a_grp", tag="a_grp", bufs=3, align_bytes=64)
            nc.vector.tensor_tensor(
                out=agg_grouped[a][:],
                in0=edge_psum[a][:].rearrange("p t b -> p b t"),
                in1=node_tiles["bias"][:],
                op=ADD,
            )

        def quantize_agg(a):
            both = quantize(agg_grouped[a][:].rearrange("p b j -> p (b j)"), NB * PACK, "a_q%d" % a)
            for g in (0, 1):
                agg_mx[a, g] = (both, slice(g * P, (g + 1) * P))

        def add_node_half(a, g):
            if g == 0:
                agg_grouped[a] = sb.tile([P, NB, PACK], BF16, name="a_grp", tag="a_grp", bufs=3, align_bytes=64)
            nc.vector.tensor_tensor(
                out=agg_grouped[a][:, g * P : (g + 1) * P, :],
                in0=edge_psum[a][:, :, g * P : (g + 1) * P].rearrange("p t b -> p b t"),
                in1=node_tiles["bias"][:, g * P : (g + 1) * P, :],
                op=ADD,
            )

        def quantize_agg_half(a, g):
            half = agg_grouped[a][:, g * P : (g + 1) * P, :].rearrange("p b j -> p (b j)")
            agg_mx[a, g] = (quantize(half, P * PACK, "a_q%d%d" % (a, g)), slice(0, P))


        def proj_tile(a):
            if a not in f_grouped:
                f_grouped[a] = sb.tile([P, NR, PACK], BF16, name="f_grp", tag="f_grp", bufs=2, align_bytes=64)
            return f_grouped[a]

        def interleave_copy(a, engine_copy, r0, r1):
            engine_copy(
                out=proj_tile(a)[:, r0:r1, :].rearrange("p (c i) j -> p c j i", i=4),
                in_=f_raw[a][:, :, r0:r1].rearrange("p j (c i) -> p c j i", i=4),
            )

        def proj_parts(a, engine):
            return [(r0, r1) for who, r0, r1 in PARTS[a] if who == engine]

        def proj_gpsimd(a):
            for r0, r1 in proj_parts(a, "gpsimd"):
                nc.gpsimd.tensor_scalar(
                    out=proj_tile(a)[:, r0:r1, :],
                    in0=f_raw[a][:, :, r0:r1].rearrange("p j r -> p r j"),
                    scalar1=1.0,
                    scalar2=0.0,
                    op0=MULT,
                    op1=ADD,
                )

        def proj_tensor(a):
            for r0, r1 in proj_parts(a, "tensor"):
                f_bank[a] = ps.tile([P, r1 - r0, PACK], BF16, name="f_bank", tag="fi", bufs=1)
                for h in range(0, r1 - r0, P):
                    nc.tensor.matmul(
                        out=f_bank[a][:, h : h + P, :].rearrange("p r j -> p j r"),
                        lhsT=ident_bf[:],
                        rhs=f_raw[a][:, :, r0 + h : r0 + h + P],
                        start=True,
                        stop=True,
                    )

        def proj_vector(a):
            for r0, r1 in proj_parts(a, "vector"):
                interleave_copy(a, nc.vector.tensor_copy, r0, r1)

        def proj_scalar(a):
            for r0, r1 in proj_parts(a, "tensor"):
                nc.scalar.copy(
                    out=proj_tile(a)[:, r0:r1, :].rearrange("p r j -> p (r j)").bitcast(F32),
                    in_=f_bank[a][:].rearrange("p r j -> p (r j)").bitcast(F32),
                )
            for r0, r1 in proj_parts(a, "scalar"):
                interleave_copy(a, nc.scalar.copy, r0, r1)

        def quantize_proj(a):
            f_mx[a] = quantize(f_grouped[a][:].rearrange("p r j -> p (r j)"), NR * PACK, "f_q%d" % a)


        def out_pass(a, g):
            if a not in (4, 6):
                out_psum[a, g] = ps.tile([P, NR], F32, name="o_bank", tag="s2", bufs=2)
            else:
                out_psum[a, g] = ps.tile([P, NR], F32, name="o_last", tag="tp", bufs=3)
            one_pass(out_psum[a, g][:], agg_mx[a, g][0], agg_mx[a, g][1], f_mx[a], slice(0, NR))

        def copy_and_store(a):
            out_sb[a] = sb.tile([P, 2, NR], F32, name="o_st", tag="o_st", bufs=4)
            if a < NA - 2:
                for g in (0, 1):
                    nc.scalar.copy(out=out_sb[a][:, g, :], in_=out_psum[a, g][:])
                nc.sync.dma_start(out=out_view[:, :, a, :], in_=out_sb[a][:])
            else:
                for g in (0, 1):
                    if a == NA - 1 and g == 0:
                        nc.vector.tensor_copy(out=out_sb[a][:, g, :], in_=out_psum[a, g][:])
                    else:
                        nc.scalar.copy(out=out_sb[a][:, g, :], in_=out_psum[a, g][:])
                    nc.sync.dma_start(out=out_view[:, g, a, :], in_=out_sb[a][:, g, :])

        for t in range(PACK):
            load_weights(t)
        load_image()
        load_edges(0)
        load_proj(0)
        load_proj(1)
        for i in (1, 2, 3):
            load_edges(i)
            load_proj(2 * i)
            load_proj(2 * i + 1)

        for t in range(PACK):
            transpose_weights(t)
            copy_weights(t)
            quantize_weights(t)
        transpose_image()
        copy_image()
        quantize_image()
        transpose_edges(0)
        copy_edges(0)
        transpose_edges(1)
        copy_edges(1)
        node_passes()
        proj_vector(0)
        proj_scalar(0)
        quantize_edges(0)
        edge_passes(0)
        transpose_edges(2)
        transpose_edges(3)
        proj_vector(1)
        proj_scalar(1)
        node_plus_bias()
        quantize_edges(1)
        edge_passes(1)
        copy_edges(2)
        quantize_proj(0)
        proj_tensor(2)

        for a in range(NA - 1):
            add_node(a)
            if a + 2 < NA:
                proj_gpsimd(a + 2)
                quantize_edges(a + 2)
                edge_passes(a + 2)
                proj_vector(a + 2)
            if a == NA - 2:
                quantize_proj(NA - 1)
            quantize_agg(a)
            out_pass(a, 0)
            out_pass(a, 1)
            if a + 3 < NA:
                copy_edges(a + 3)
            if a + 2 < NA:
                proj_scalar(a + 2)
            if a + 3 < NA:
                proj_tensor(a + 3)
            if a % 2 == 0 and a + 4 < NA:
                transpose_edges(a + 4)
                transpose_edges(a + 5)
            copy_and_store(a)
            if a + 1 < NA - 1:
                quantize_proj(a + 1)

        add_node_half(NA - 1, 0)
        add_node_half(NA - 1, 1)
        quantize_agg_half(NA - 1, 0)
        out_pass(NA - 1, 0)
        quantize_agg_half(NA - 1, 1)
        out_pass(NA - 1, 1)
        copy_and_store(NA - 1)
